import numpy as np
import ml_dtypes


def mxq(x, axis, fmt="e4m3"):
    dtype, down = {"e4m3": (ml_dtypes.float8_e4m3fn, 7), "e5m2": (ml_dtypes.float8_e5m2, 14)}[fmt]
    v = np.moveaxis(np.asarray(x, np.float32).astype(ml_dtypes.bfloat16).astype(np.float64), axis, -1)
    blocks = v.reshape(v.shape[:-1] + (-1, 32))
    amax = np.abs(blocks).max(-1, keepdims=True)
    byte = np.maximum(np.where(amax > 0, np.frexp(amax)[1] - 1 + 127, 0) - down, 1)
    scale = np.exp2(byte - 127.0)
    codes = (blocks / scale).astype(np.float32).astype(dtype).astype(np.float64)
    return np.moveaxis((codes * scale).reshape(v.shape), -1, axis)


WIDE = False


def mx_kscale(k):
    if not WIDE:
        return np.ones(k)
    levels = np.array([10, -10, 5, -5, 0])
    if k % 512:
        return np.exp2(np.random.permutation(np.resize(levels, k // 32))).repeat(32)
    a = np.empty((k // 512, 16))
    for p in range(k // 512):
        a[p, :8] = np.random.permutation(np.resize(levels, 8))
        for g in range(8):
            far = levels[np.abs(levels - a[p, g]) >= 10]
            a[p, g + 8] = far[np.random.randint(len(far))]
    return np.exp2(a.ravel()).repeat(32)


BF16 = ml_dtypes.bfloat16


def bf(x):
    return np.asarray(x, np.float32).astype(BF16)


def f64(x):
    return np.asarray(x).astype(np.float64)


B, T, KA, KT, DIM, NH, HD, E = 2, 512, 256, 256, 1024, 8, 128, 8
ROPE_BASE = 10000.0


def rope_cos_sin(L, hd):
    inv_freq = 1.0 / (ROPE_BASE ** (f64(np.arange(0, hd, 2)) / hd))
    freqs = f64(np.arange(L))[:, None] * inv_freq[None, :]
    emb = np.concatenate([freqs, freqs], axis=-1)
    return np.cos(emb), np.sin(emb)


def rotate_half(x):
    x1 = x[..., 0::2]
    x2 = x[..., 1::2]
    return np.stack((-x2, x1), axis=-1).reshape(x.shape)


def rope(t, cos, sin):
    return t * cos[None, None] + rotate_half(t) * sin[None, None]


def heads(t):
    return t.reshape(B, -1, NH, HD).transpose(0, 2, 1, 3)


def setup_inputs():
    s = mx_kscale(DIM)
    c = 1.2 / np.sqrt(DIM)
    return {"x": bf(np.random.standard_normal((B, T, DIM)) * s),
            "W_qa": bf(np.random.standard_normal((NH * HD, DIM)) * c / s[None, :]),
            "b_qa": bf(np.random.standard_normal(NH * HD) * 0.3),
            "W_qt": bf(np.random.standard_normal((NH * HD, DIM)) * c / s[None, :]),
            "b_qt": bf(np.random.standard_normal(NH * HD) * 0.3)}


def reference(x, W_qa, b_qa, W_qt, b_qt):
    xq = mxq(f64(x), 2, "e4m3")
    q_a = heads((xq @ mxq(f64(W_qa), 1, "e4m3").T) + f64(b_qa))
    q_t = heads((xq @ mxq(f64(W_qt), 1, "e4m3").T) + f64(b_qt))
    cos_m, sin_m = rope_cos_sin(T, HD)
    return rope(q_a, cos_m, sin_m), rope(q_t, cos_m, sin_m)

@@ -1,0 +1,268 @@
+import math
+from contextlib import ExitStack
+
+import concourse.mybir as mybir
+from concourse.masks import make_identity
+
+F32 = mybir.dt.float32
+BF16 = mybir.dt.bfloat16
+I32 = mybir.dt.int32
+U32 = mybir.dt.uint32
+U8 = mybir.dt.uint8
+FP8X4 = mybir.dt.float8_e4m3fn_x4
+ALU = mybir.AluOpType
+ACT = mybir.ActivationFunctionType
+
+P = 128
+FLOPS = 2 * 1024 * 1024 * 2048
+
+TWO_PI = 2.0 * math.pi
+C1 = 6.283203125
+C2 = TWO_PI - C1
+RATIO = 10000.0 ** (-1.0 / 64.0)
+N_ROUNDS = 16
+LAST_DIRECT = 6
+FIRST_VECTOR_ADD = 12
+
+
+def tile_l1regressionmoeactionhead_pa_kernel(tc, x, W_qa, b_qa, W_qt, b_qt, out_0, out_1):
+    nc = tc.nc
+    weights = [W_qa, W_qt]
+    outs = [out_0, out_1]
+    with ExitStack() as ctx:
+        keep = ctx.enter_context(tc.tile_pool(name="keep", bufs=1))
+        wgp = ctx.enter_context(tc.tile_pool(name="wgp", bufs=3))
+        qsp = ctx.enter_context(tc.tile_pool(name="qsp", bufs=3))
+        abp = ctx.enter_context(tc.tile_pool(name="abp", bufs=8))
+        obp = ctx.enter_context(tc.tile_pool(name="obp", bufs=4))
+        psum = ctx.enter_context(tc.psum_pool(name="psum", bufs=1))
+        ctx.enter_context(tc.manual_schedule())
+
+        def bank(tag):
+            return psum.tile([P, 512], F32, name="bk" + tag, tag=tag)
+
+        ident = keep.tile([P, P], F32, name="ident")
+        x_sb = [[keep.tile([P, 1024], BF16, name="x%d%d" % (n, j)) for j in range(4)] for n in range(2)]
+        w_sb = [keep.tile([P, 2048], BF16, name="w%d" % k) for k in range(8)]
+        xg = [keep.tile([P, 4096], BF16, name="xg%d" % n, align_bytes=64) for n in range(2)]
+        xcodes = [keep.tile([P, 1024], U32, name="xc%d" % n, align_bytes=64) for n in range(2)]
+        xscales = [keep.tile([P, 1024], U8, name="xs%d" % n, align_bytes=64) for n in range(2)]
+        wcodes = [keep.tile([P, 512], U32, name="wc%d" % k, align_bytes=64) for k in range(8)]
+        wscales = [keep.tile([P, 512], U8, name="ws%d" % k, align_bytes=64) for k in range(8)]
+        dm0 = keep.tile([P, 1], F32, name="dm0")
+        dm1 = keep.tile([P, 1], F32, name="dm1")
+        bz = keep.tile([P, 256], BF16, name="bz")
+        bf = keep.tile([P, 2, P], F32, name="bf")
+        bias_sb = keep.tile([P, 2, 8], F32, name="bias_sb")
+        freq = keep.tile([P, 64], F32, name="freq")
+        t_i = keep.tile([P, 4], I32, name="t_i")
+        t_f = keep.tile([P, 4], F32, name="t_f")
+        ang = keep.tile([P, 4, 64], F32, name="ang")
+        k_i = keep.tile([P, 4, 64], I32, name="k_i")
+        k_f = keep.tile([P, 4, 64], F32, name="k_f")
+        r1 = keep.tile([P, 4, 64], F32, name="r1")
+        r2 = keep.tile([P, 4, 64], F32, name="r2")
+        gs = keep.tile([P, 4, 64], F32, name="gs")
+        gc = keep.tile([P, 4, 64], F32, name="gc")
+        rs = keep.tile([P, 4, 64], F32, name="rs")
+        rc = keep.tile([P, 4, 64], F32, name="rc")
+        cos_t = keep.tile([P, 2, 4, 2, 32], F32, name="cos_t")
+        sin_t = keep.tile([P, 2, 4, 2, 32], F32, name="sin_t")
+
+        make_identity(nc, ident[:])
+        nc.gpsimd.iota(t_i[:], pattern=[[1, 4]], base=0, channel_multiplier=4)
+        nc.vector.memset(dm0[:], 0.0)
+        nc.vector.memset(bz[:], 0.0)
+        nc.vector.memset(freq[:, 0:1], 1.0)
+
+        nc.scalar.dma_start(out=bz[0:4, :], in_=b_qa.rearrange("(r c) -> r c", c=256))
+        nc.scalar.dma_start(out=bz[4:8, :], in_=b_qt.rearrange("(r c) -> r c", c=256))
+
+        def load_w(k):
+            rows = weights[k // 4][256 * (k % 4):256 * (k % 4) + 256, :]
+            nc.sync.dma_start(out=w_sb[k][:], in_=rows.rearrange("(p m) k -> p (m k)", m=2))
+
+        def load_x(n):
+            view = x[n].rearrange("(p j) k -> p j k", j=4)
+            for j in range(4):
+                nc.sync.dma_start(out=x_sb[n][j][:], in_=view[:, j, :])
+
+        load_w(0)
+        load_x(0)
+        load_w(1)
+        load_x(1)
+        for k in range(2, 8):
+            load_w(k)
+
+        nc.scalar.activation(out=dm1[:], in_=dm0[:], func=ACT.Sin)
+
+        for c in range(1, 4):
+            nc.vector.tensor_scalar(out=freq[:, c:c + 1], in0=freq[:, 0:1], scalar1=RATIO ** c,
+                                    scalar2=None, op0=ALU.mult)
+        for a in range(1, 4):
+            nc.vector.tensor_scalar(out=freq[:, 4 * a:4 * a + 4], in0=freq[:, 0:4], scalar1=RATIO ** (4 * a),
+                                    scalar2=None, op0=ALU.mult)
+        for a in range(1, 4):
+            nc.vector.tensor_scalar(out=freq[:, 16 * a:16 * a + 16], in0=freq[:, 0:16], scalar1=RATIO ** (16 * a),
+                                    scalar2=None, op0=ALU.mult)
+        nc.vector.tensor_copy(out=t_f[:], in_=t_i[:])
+        nc.vector.tensor_tensor(out=ang[:], in0=freq[:].unsqueeze(1).to_broadcast([P, 4, 64]),
+                                in1=t_f[:].unsqueeze(2).to_broadcast([P, 4, 64]), op=ALU.mult)
+        nc.vector.tensor_scalar(out=k_i[:], in0=ang[:], scalar1=1.0 / TWO_PI, scalar2=None, op0=ALU.mult)
+        nc.vector.tensor_copy(out=k_f[:], in_=k_i[:])
+        nc.vector.tensor_copy(out=bf[:], in_=bz[:].rearrange("r (p m) -> r m p", m=2))
+        nc.vector.scalar_tensor_tensor(out=r1[:], in0=k_f[:], scalar=-C1, in1=ang[:], op0=ALU.mult, op1=ALU.add)
+        nc.vector.scalar_tensor_tensor(out=r2[:], in0=k_f[:], scalar=-C2, in1=r1[:], op0=ALU.mult, op1=ALU.add)
+
+        def words_in(src32, tag):
+            bk = bank(tag)
+            for q in range(4):
+                first = 2 * P * (q // 2) + q % 2
+                nc.tensor.transpose(bk[:, P * q:P * (q + 1)], src32[:, first:first + 2 * P - 1:2], ident[:])
+            return bk[:].rearrange("p (g u r) -> p g r u", g=2, u=2)
+
+        wg = {}
+
+        def w_in(k, m, tag):
+            if m == 0:
+                wg[k] = wgp.tile([P, 2048], BF16, name="wg", align_bytes=64)
+            src = words_in(w_sb[k][:].bitcast(F32)[:, 512 * m:512 * (m + 1)], tag)
+            dst = wg[k][:].bitcast(F32)[:, 512 * m:512 * (m + 1)].rearrange("p (g r u) -> p g r u", g=2, u=2)
+            nc.scalar.copy(out=dst, in_=src)
+
+        def w_quant(k):
+            nc.vector.quantize_mx(out=wcodes[k][:].bitcast(FP8X4), scales=wscales[k][:], in_=wg[k][:])
+
+        def x_in(n, j, tag):
+            src = words_in(x_sb[n][j][:].bitcast(F32), tag)
+            dst = xg[n][:].bitcast(F32).rearrange("p (g c u) -> p g c u", g=2, u=2)[:, :, P * j:P * (j + 1), :]
+            nc.scalar.copy(out=dst, in_=src)
+
+        def x_quant(n, j):
+            for g in range(2):
+                c0 = 512 * g + P * j
+                nc.vector.quantize_mx(out=xcodes[n][:, c0:c0 + P].bitcast(FP8X4), scales=xscales[n][:, c0:c0 + P],
+                                      in_=xg[n][:, 4 * c0:4 * (c0 + P)])
+
+        rounds = [(0, 0), (1, 0), (0, 1), (1, 1)] + [(k, n) for k in range(2, 8) for n in range(2)]
+        acc = {}
+        qs = {}
+        tb = {}
+        ab = {}
+
+        def mx(i):
+            k, n = rounds[i]
+            spare = i > LAST_DIRECT and i % 2 == 0
+            for m in range(2):
+                acc[(i, m)] = bank(("IN%d" if spare else "ACC%d") % m)
+                for g in range(2):
+                    s0 = P * (2 * m + g)
+                    nc.tensor.matmul_mx(out=acc[(i, m)][:],
+                                        lhsT=wcodes[k][:, s0:s0 + P].bitcast(FP8X4),
+                                        lhsT_scale=wscales[k][:, s0:s0 + P],
+                                        rhs=xcodes[n][:, 512 * g:512 * (g + 1)].bitcast(FP8X4),
+                                        rhs_scale=xscales[n][:, 512 * g:512 * (g + 1)],
+                                        start=(g == 0), stop=(g == 1))
+            for m in range(2):
+                qs[(i, m)] = qsp.tile([P, 512], F32, name="qs%d" % m)
+                nc.scalar.activation(out=qs[(i, m)][:], in_=acc[(i, m)][:], func=ACT.Identity,
+                                     bias=bias_sb[:, m, k:k + 1], scale=1.0)
+
+        ident_hc = ident[:].rearrange("p (h c) -> p h c", h=2)
+
+        def back(i):
+            for m in range(2):
+                tb[(i, m)] = bank("T%d%d" % (i % 2, m))
+                by_head = tb[(i, m)][:].rearrange("p (h j c) -> p h j c", h=2, j=4)
+                for j in range(4):
+                    nc.tensor.transpose(by_head[:, :, j, :], qs[(i, m)][:, P * j:P * (j + 1)], ident_hc)
+
+        def rope(i, tiles=(0, 1)):
+            if 0 in tiles:
+                ab[i] = abp.tile([P, 2, 2, 512], F32, name="ab")
+            for m in tiles:
+                tv = tb[(i, m)][:].rearrange("p (h c) -> p h c", h=2)
+                cos_v = cos_t[:, m].rearrange("p j r c -> p (j r c)").unsqueeze(1).to_broadcast([P, 2, 256])
+                sin_v = sin_t[:, 1 - m].rearrange("p j r c -> p (j r c)").unsqueeze(1).to_broadcast([P, 2, 256])
+                nc.vector.tensor_tensor(out=ab[i][:, 0, m, :].rearrange("p (h c) -> p h c", h=2), in0=tv,
+                                        in1=cos_v, op=ALU.mult)
+                nc.vector.tensor_tensor(out=ab[i][:, 1, 1 - m, :].rearrange("p (h c) -> p h c", h=2), in0=tv,
+                                        in1=sin_v, op=ALU.mult)
+
+        def add_store(i):
+            k, n = rounds[i]
+            head = 2 * (k % 4)
+            dst = outs[k // 4][n, head:head + 2].rearrange("h (p j) d -> p h (j d)", j=4)
+            ob = obp.tile([P, 2, 512], F32, name="ob")
+            a_v = ab[i][:, 0].rearrange("p e c -> p c e")
+            b_v = ab[i][:, 1].rearrange("p e c -> p c e")
+            o_v = ob[:].rearrange("p h (c e) -> p (h c) e", e=2)
+            if i < FIRST_VECTOR_ADD:
+                nc.gpsimd.tensor_tensor(out=o_v, in0=a_v, in1=b_v, op=ALU.add)
+                nc.sync.dma_start(out=dst, in_=ob[:])
+            else:
+                for h in range(2):
+                    cols = slice(256 * h, 256 * (h + 1))
+                    nc.vector.tensor_tensor(out=o_v[:, cols, :], in0=a_v[:, cols, :], in1=b_v[:, cols, :], op=ALU.add)
+                    nc.sync.dma_start(out=dst[:, h, :], in_=ob[:, h, :])
+
+        w_in(0, 0, "IN0")
+        w_in(0, 1, "IN1")
+        for j in range(4):
+            x_in(0, j, "T%d%d" % (j // 2, j % 2))
+            if j == 0:
+                w_quant(0)
+            else:
+                x_quant(0, j - 1)
+        x_quant(0, 3)
+        nc.vector.tensor_scalar(out=gs[:], in0=r2[:], scalar1=math.pi, scalar2=-TWO_PI, op0=ALU.is_gt, op1=ALU.mult)
+        nc.vector.tensor_scalar(out=gc[:], in0=r2[:], scalar1=0.5 * math.pi, scalar2=-TWO_PI,
+                                op0=ALU.is_gt, op1=ALU.mult)
+        nc.vector.tensor_tensor(out=rs[:], in0=r2[:], in1=gs[:], op=ALU.add)
+        nc.vector.scalar_tensor_tensor(out=rc[:], in0=r2[:], scalar=0.5 * math.pi, in1=gc[:],
+                                       op0=ALU.add, op1=ALU.add)
+        bias_ps = bank("ACC1")
+        for m in range(2):
+            nc.tensor.transpose(bias_ps[:, P * m:P * (m + 1)], bf[:, m, :], ident[:])
+        nc.scalar.copy(out=bias_sb[:], in_=bias_ps[:, 0:256].rearrange("p (m r) -> p m r", m=2)[:, :, 0:8])
+        w_in(1, 0, "IN0")
+        w_in(1, 1, "IN1")
+        w_quant(1)
+        for e in range(2):
+            rc_v = rc[:].rearrange("p j (c e) -> p e j c", e=2)[:, e].unsqueeze(2).to_broadcast([P, 4, 2, 32])
+            rs_v = rs[:].rearrange("p j (c e) -> p e j c", e=2)[:, e].unsqueeze(2).to_broadcast([P, 4, 2, 32])
+            nc.scalar.activation(out=cos_t[:, e], in_=rc_v, func=ACT.Sin)
+            nc.scalar.activation(out=sin_t[:, e], in_=rs_v, func=ACT.Sin, scale=(-1.0 if e == 0 else 1.0))
+        mx(0)
+        x_in(1, 0, "T10")
+        x_in(1, 1, "T11")
+        x_in(1, 2, "IN0")
+        x_in(1, 3, "IN1")
+        back(0)
+        x_quant(1, 0)
+        x_quant(1, 1)
+        rope(0, (0,))
+        x_quant(1, 2)
+        x_quant(1, 3)
+        rope(0, (1,))
+        add_store(0)
+
+        for r in range(1, LAST_DIRECT + 1):
+            mx(r)
+            w_in(r + 1, 0, "IN0")
+            w_in(r + 1, 1, "IN1")
+            back(r)
+            rope(r)
+            add_store(r)
+            w_quant(r + 1)
+        mx(LAST_DIRECT + 1)
+        for r in range(LAST_DIRECT + 2, N_ROUNDS):
+            mx(r)
+            back(r - 1)
+            rope(r - 1)
+            if r - 1 < FIRST_VECTOR_ADD:
+                add_store(r - 1)
+        back(N_ROUNDS - 1)
+        rope(N_ROUNDS - 1)
+        for r in range(FIRST_VECTOR_ADD, N_ROUNDS):
+            add_store(r)

@@ -66,8 +66,7 @@ def tile_l1regressionmoeactionhead_pa_kernel(tc, x, W_qa, b_qa, W_qt, b_qt, out_
         gc = keep.tile([P, 4, 64], F32, name="gc")
         rs = keep.tile([P, 4, 64], F32, name="rs")
         rc = keep.tile([P, 4, 64], F32, name="rc")
-        cos_t = keep.tile([P, 2, 4, 2, 32], F32, name="cos_t")
-        sin_t = keep.tile([P, 2, 4, 2, 32], F32, name="sin_t")
+        rope_t = keep.tile([P, 2, 2, 4, 2, 32], F32, name="rope_t")
 
         make_identity(nc, ident[:])
         nc.gpsimd.iota(t_i[:], pattern=[[1, 4]], base=0, channel_multiplier=4)
@@ -181,13 +180,10 @@ def tile_l1regressionmoeactionhead_pa_kernel(tc, x, W_qa, b_qa, W_qt, b_qt, out_
             if 0 in tiles:
                 ab[i] = abp.tile([P, 2, 2, 512], F32, name="ab")
             for m in tiles:
-                tv = tb[(i, m)][:].rearrange("p (h c) -> p h c", h=2)
-                cos_v = cos_t[:, m].rearrange("p j r c -> p (j r c)").unsqueeze(1).to_broadcast([P, 2, 256])
-                sin_v = sin_t[:, 1 - m].rearrange("p j r c -> p (j r c)").unsqueeze(1).to_broadcast([P, 2, 256])
-                nc.vector.tensor_tensor(out=ab[i][:, 0, m, :].rearrange("p (h c) -> p h c", h=2), in0=tv,
-                                        in1=cos_v, op=ALU.mult)
-                nc.vector.tensor_tensor(out=ab[i][:, 1, 1 - m, :].rearrange("p (h c) -> p h c", h=2), in0=tv,
-                                        in1=sin_v, op=ALU.mult)
+                tv = tb[(i, m)][:].rearrange("p (h c) -> p h c", h=2).unsqueeze(1).to_broadcast([P, 2, 2, 256])
+                tab_v = rope_t[:, m].rearrange("p e j r c -> p e (j r c)").unsqueeze(2).to_broadcast([P, 2, 2, 256])
+                nc.vector.tensor_tensor(out=ab[i][:, m].rearrange("p e (h c) -> p e h c", h=2), in0=tv,
+                                        in1=tab_v, op=ALU.mult)
 
         def add_store(i):
             k, n = rounds[i]
@@ -231,8 +227,8 @@ def tile_l1regressionmoeactionhead_pa_kernel(tc, x, W_qa, b_qa, W_qt, b_qt, out_
         for e in range(2):
             rc_v = rc[:].rearrange("p j (c e) -> p e j c", e=2)[:, e].unsqueeze(2).to_broadcast([P, 4, 2, 32])
             rs_v = rs[:].rearrange("p j (c e) -> p e j c", e=2)[:, e].unsqueeze(2).to_broadcast([P, 4, 2, 32])
-            nc.scalar.activation(out=cos_t[:, e], in_=rc_v, func=ACT.Sin)
-            nc.scalar.activation(out=sin_t[:, e], in_=rs_v, func=ACT.Sin, scale=(-1.0 if e == 0 else 1.0))
+            nc.scalar.activation(out=rope_t[:, e, e], in_=rc_v, func=ACT.Sin)
+            nc.scalar.activation(out=rope_t[:, 1 - e, e], in_=rs_v, func=ACT.Sin, scale=(-1.0 if e == 0 else 1.0))
         mx(0)
         x_in(1, 0, "T10")
         x_in(1, 1, "T11")

@@ -20,21 +20,19 @@ TWO_PI = 2.0 * math.pi
 C1 = 6.283203125
 C2 = TWO_PI - C1
 RATIO = 10000.0 ** (-1.0 / 64.0)
-N_ROUNDS = 16
-LAST_DIRECT = 6
-FIRST_VECTOR_ADD = 12
 
 
 def tile_l1regressionmoeactionhead_pa_kernel(tc, x, W_qa, b_qa, W_qt, b_qt, out_0, out_1):
     nc = tc.nc
     weights = [W_qa, W_qt]
     outs = [out_0, out_1]
+    V, S, G = nc.vector, nc.scalar, nc.gpsimd
     with ExitStack() as ctx:
         keep = ctx.enter_context(tc.tile_pool(name="keep", bufs=1))
         wgp = ctx.enter_context(tc.tile_pool(name="wgp", bufs=3))
+        abp = ctx.enter_context(tc.tile_pool(name="abp", bufs=6))
         qsp = ctx.enter_context(tc.tile_pool(name="qsp", bufs=3))
-        abp = ctx.enter_context(tc.tile_pool(name="abp", bufs=8))
-        obp = ctx.enter_context(tc.tile_pool(name="obp", bufs=4))
+        obp = ctx.enter_context(tc.tile_pool(name="obp", bufs=6))
         psum = ctx.enter_context(tc.psum_pool(name="psum", bufs=1))
         ctx.enter_context(tc.manual_schedule())
 
@@ -42,18 +40,20 @@ def tile_l1regressionmoeactionhead_pa_kernel(tc, x, W_qa, b_qa, W_qt, b_qt, out_
             return psum.tile([P, 512], F32, name="bk" + tag, tag=tag)
 
         ident = keep.tile([P, P], F32, name="ident")
+        swap = keep.tile([P, P], F32, name="swap")
         x_sb = [[keep.tile([P, 1024], BF16, name="x%d%d" % (n, j)) for j in range(4)] for n in range(2)]
-        w_sb = [keep.tile([P, 2048], BF16, name="w%d" % k) for k in range(8)]
-        xg = [keep.tile([P, 4096], BF16, name="xg%d" % n, align_bytes=64) for n in range(2)]
+        w_sb = [[keep.tile([P, 1024], BF16, name="w%d%d" % (k, m)) for m in range(2)] for k in range(8)]
+        xg = [[keep.tile([P, 1024], BF16, name="xg%d%d" % (n, j), align_bytes=64) for j in range(4)] for n in range(2)]
         xcodes = [keep.tile([P, 1024], U32, name="xc%d" % n, align_bytes=64) for n in range(2)]
         xscales = [keep.tile([P, 1024], U8, name="xs%d" % n, align_bytes=64) for n in range(2)]
         wcodes = [keep.tile([P, 512], U32, name="wc%d" % k, align_bytes=64) for k in range(8)]
         wscales = [keep.tile([P, 512], U8, name="ws%d" % k, align_bytes=64) for k in range(8)]
         dm0 = keep.tile([P, 1], F32, name="dm0")
         dm1 = keep.tile([P, 1], F32, name="dm1")
-        bz = keep.tile([P, 256], BF16, name="bz")
-        bf = keep.tile([P, 2, P], F32, name="bf")
-        bias_sb = keep.tile([P, 2, 8], F32, name="bias_sb")
+        half_pi = keep.tile([P, 1], F32, name="half_pi")
+        bz = keep.tile([P, P], BF16, name="bz")
+        bf = keep.tile([P, P], F32, name="bf")
+        bias_sb = keep.tile([P, 16], F32, name="bias_sb")
         freq = keep.tile([P, 64], F32, name="freq")
         t_i = keep.tile([P, 4], I32, name="t_i")
         t_f = keep.tile([P, 4], F32, name="t_f")
@@ -66,34 +66,45 @@ def tile_l1regressionmoeactionhead_pa_kernel(tc, x, W_qa, b_qa, W_qt, b_qt, out_
         gc = keep.tile([P, 4, 64], F32, name="gc")
         rs = keep.tile([P, 4, 64], F32, name="rs")
         rc = keep.tile([P, 4, 64], F32, name="rc")
-        rope_t = keep.tile([P, 2, 2, 4, 2, 32], F32, name="rope_t")
+        tok = keep.tile([P, 2, 4, 2, 64], F32, name="tok")
+        chan = keep.tile([P, 2, 512], F32, name="chan")
 
         make_identity(nc, ident[:])
         nc.gpsimd.iota(t_i[:], pattern=[[1, 4]], base=0, channel_multiplier=4)
-        nc.vector.memset(dm0[:], 0.0)
         nc.vector.memset(bz[:], 0.0)
+        nc.vector.memset(dm0[:], 0.0)
         nc.vector.memset(freq[:, 0:1], 1.0)
 
-        nc.scalar.dma_start(out=bz[0:4, :], in_=b_qa.rearrange("(r c) -> r c", c=256))
-        nc.scalar.dma_start(out=bz[4:8, :], in_=b_qt.rearrange("(r c) -> r c", c=256))
+        nc.scalar.dma_start(out=bz[0:8, :], in_=b_qa.rearrange("(r c) -> r c", c=P))
+        nc.scalar.dma_start(out=bz[8:16, :], in_=b_qt.rearrange("(r c) -> r c", c=P))
 
-        def load_w(k):
-            rows = weights[k // 4][256 * (k % 4):256 * (k % 4) + 256, :]
-            nc.sync.dma_start(out=w_sb[k][:], in_=rows.rearrange("(p m) k -> p (m k)", m=2))
+        def load_w(k, m):
+            row0 = 256 * (k % 4) + P * m
+            nc.sync.dma_start(out=w_sb[k][m][:], in_=weights[k // 4][row0:row0 + P, :])
 
-        def load_x(n):
-            view = x[n].rearrange("(p j) k -> p j k", j=4)
-            for j in range(4):
-                nc.sync.dma_start(out=x_sb[n][j][:], in_=view[:, j, :])
+        def load_x(n, j):
+            nc.sync.dma_start(out=x_sb[n][j][:], in_=x[n].rearrange("(p j) k -> p j k", j=4)[:, j, :])
 
-        load_w(0)
-        load_x(0)
-        load_w(1)
-        load_x(1)
+        for j in range(2):
+            load_x(0, j)
+        for m in range(2):
+            load_w(0, m)
+        for j in range(2, 4):
+            load_x(0, j)
+        for m in range(2):
+            load_w(1, m)
+        for j in range(4):
+            load_x(1, j)
         for k in range(2, 8):
-            load_w(k)
+            for m in range(2):
+                load_w(k, m)
 
         nc.scalar.activation(out=dm1[:], in_=dm0[:], func=ACT.Sin)
+
+        swap_v = swap[:].rearrange("p (c e) -> p c e", e=2)
+        ident_v = ident[:].rearrange("p (c e) -> p c e", e=2)
+        for e in range(2):
+            nc.gpsimd.tensor_copy(out=swap_v[:, :, e], in_=ident_v[:, :, 1 - e])
 
         for c in range(1, 4):
             nc.vector.tensor_scalar(out=freq[:, c:c + 1], in0=freq[:, 0:1], scalar1=RATIO ** c,
@@ -101,6 +112,7 @@ def tile_l1regressionmoeactionhead_pa_kernel(tc, x, W_qa, b_qa, W_qt, b_qt, out_
         for a in range(1, 4):
             nc.vector.tensor_scalar(out=freq[:, 4 * a:4 * a + 4], in0=freq[:, 0:4], scalar1=RATIO ** (4 * a),
                                     scalar2=None, op0=ALU.mult)
+        nc.vector.tensor_scalar(out=half_pi[:], in0=freq[:, 0:1], scalar1=0.5 * math.pi, scalar2=None, op0=ALU.mult)
         for a in range(1, 4):
             nc.vector.tensor_scalar(out=freq[:, 16 * a:16 * a + 16], in0=freq[:, 0:16], scalar1=RATIO ** (16 * a),
                                     scalar2=None, op0=ALU.mult)
@@ -109,9 +121,17 @@ def tile_l1regressionmoeactionhead_pa_kernel(tc, x, W_qa, b_qa, W_qt, b_qt, out_
                                 in1=t_f[:].unsqueeze(2).to_broadcast([P, 4, 64]), op=ALU.mult)
         nc.vector.tensor_scalar(out=k_i[:], in0=ang[:], scalar1=1.0 / TWO_PI, scalar2=None, op0=ALU.mult)
         nc.vector.tensor_copy(out=k_f[:], in_=k_i[:])
-        nc.vector.tensor_copy(out=bf[:], in_=bz[:].rearrange("r (p m) -> r m p", m=2))
         nc.vector.scalar_tensor_tensor(out=r1[:], in0=k_f[:], scalar=-C1, in1=ang[:], op0=ALU.mult, op1=ALU.add)
         nc.vector.scalar_tensor_tensor(out=r2[:], in0=k_f[:], scalar=-C2, in1=r1[:], op0=ALU.mult, op1=ALU.add)
+        nc.vector.tensor_scalar(out=gc[:], in0=r2[:], scalar1=0.5 * math.pi, scalar2=-TWO_PI,
+                                op0=ALU.is_gt, op1=ALU.mult)
+        nc.vector.tensor_scalar(out=gs[:], in0=r2[:], scalar1=math.pi, scalar2=TWO_PI, op0=ALU.is_gt, op1=ALU.mult)
+        nc.vector.tensor_tensor(out=rc[:], in0=r2[:], in1=gc[:], op=ALU.add)
+        r2_v = r2[:].rearrange("p j (c e) -> p j c e", e=2)
+        gs_v = gs[:].rearrange("p j (c e) -> p j c e", e=2)
+        rs_v = rs[:].rearrange("p j (c e) -> p j c e", e=2)
+        nc.gpsimd.tensor_tensor(out=rs_v[:, :, :, 0], in0=r2_v[:, :, :, 1], in1=gs_v[:, :, :, 1], op=ALU.subtract)
+        nc.gpsimd.tensor_tensor(out=rs_v[:, :, :, 1], in0=gs_v[:, :, :, 0], in1=r2_v[:, :, :, 0], op=ALU.subtract)
 
         def words_in(src32, tag):
             bk = bank(tag)
@@ -120,145 +140,173 @@ def tile_l1regressionmoeactionhead_pa_kernel(tc, x, W_qa, b_qa, W_qt, b_qt, out_
                 nc.tensor.transpose(bk[:, P * q:P * (q + 1)], src32[:, first:first + 2 * P - 1:2], ident[:])
             return bk[:].rearrange("p (g u r) -> p g r u", g=2, u=2)
 
+        def copy_out(eng, out, in_):
+            if eng is nc.scalar:
+                nc.scalar.copy(out=out, in_=in_)
+            else:
+                nc.vector.tensor_copy(out=out, in_=in_)
+
         wg = {}
 
-        def w_in(k, m, tag):
+        def w_in(k, m, tag, eng):
             if m == 0:
                 wg[k] = wgp.tile([P, 2048], BF16, name="wg", align_bytes=64)
-            src = words_in(w_sb[k][:].bitcast(F32)[:, 512 * m:512 * (m + 1)], tag)
+            src = words_in(w_sb[k][m][:].bitcast(F32), tag)
             dst = wg[k][:].bitcast(F32)[:, 512 * m:512 * (m + 1)].rearrange("p (g r u) -> p g r u", g=2, u=2)
-            nc.scalar.copy(out=dst, in_=src)
+            copy_out(eng, dst, src)
 
         def w_quant(k):
             nc.vector.quantize_mx(out=wcodes[k][:].bitcast(FP8X4), scales=wscales[k][:], in_=wg[k][:])
 
-        def x_in(n, j, tag):
+        def w_quant_half(k, m):
+            c0 = 256 * m
+            nc.vector.quantize_mx(out=wcodes[k][:, c0:c0 + 256].bitcast(FP8X4), scales=wscales[k][:, c0:c0 + 256],
+                                  in_=wg[k][:, 4 * c0:4 * (c0 + 256)])
+
+        def x_in(n, j, tag, eng):
             src = words_in(x_sb[n][j][:].bitcast(F32), tag)
-            dst = xg[n][:].bitcast(F32).rearrange("p (g c u) -> p g c u", g=2, u=2)[:, :, P * j:P * (j + 1), :]
-            nc.scalar.copy(out=dst, in_=src)
+            copy_out(eng, xg[n][j][:].bitcast(F32).rearrange("p (g c u) -> p g c u", g=2, u=2), src)
 
         def x_quant(n, j):
             for g in range(2):
                 c0 = 512 * g + P * j
                 nc.vector.quantize_mx(out=xcodes[n][:, c0:c0 + P].bitcast(FP8X4), scales=xscales[n][:, c0:c0 + P],
-                                      in_=xg[n][:, 4 * c0:4 * (c0 + P)])
+                                      in_=xg[n][j][:, 512 * g:512 * (g + 1)])
 
         rounds = [(0, 0), (1, 0), (0, 1), (1, 1)] + [(k, n) for k in range(2, 8) for n in range(2)]
         acc = {}
-        qs = {}
-        tb = {}
-        ab = {}
+        prod = {}
+        ob = {}
 
-        def mx(i):
-            k, n = rounds[i]
-            spare = i > LAST_DIRECT and i % 2 == 0
-            for m in range(2):
-                acc[(i, m)] = bank(("IN%d" if spare else "ACC%d") % m)
-                for g in range(2):
-                    s0 = P * (2 * m + g)
-                    nc.tensor.matmul_mx(out=acc[(i, m)][:],
-                                        lhsT=wcodes[k][:, s0:s0 + P].bitcast(FP8X4),
-                                        lhsT_scale=wscales[k][:, s0:s0 + P],
-                                        rhs=xcodes[n][:, 512 * g:512 * (g + 1)].bitcast(FP8X4),
-                                        rhs_scale=xscales[n][:, 512 * g:512 * (g + 1)],
-                                        start=(g == 0), stop=(g == 1))
-            for m in range(2):
-                qs[(i, m)] = qsp.tile([P, 512], F32, name="qs%d" % m)
-                nc.scalar.activation(out=qs[(i, m)][:], in_=acc[(i, m)][:], func=ACT.Identity,
-                                     bias=bias_sb[:, m, k:k + 1], scale=1.0)
+        def mx(r, m):
+            k, n = rounds[r]
+            acc[(r, m)] = bank("A%d%d" % (r % 2, m))
+            for g in range(2):
+                s0 = P * (2 * m + g)
+                nc.tensor.matmul_mx(out=acc[(r, m)][:],
+                                    lhsT=wcodes[k][:, s0:s0 + P].bitcast(FP8X4), lhsT_scale=wscales[k][:, s0:s0 + P],
+                                    rhs=xcodes[n][:, 512 * g:512 * (g + 1)].bitcast(FP8X4),
+                                    rhs_scale=xscales[n][:, 512 * g:512 * (g + 1)],
+                                    start=(g == 0), stop=(g == 1))
 
-        ident_hc = ident[:].rearrange("p (h c) -> p h c", h=2)
+        def bias_of(r, m):
+            head = 2 * rounds[r][0] + m
+            return bias_sb[:, head:head + 1]
 
-        def back(i):
-            for m in range(2):
-                tb[(i, m)] = bank("T%d%d" % (i % 2, m))
-                by_head = tb[(i, m)][:].rearrange("p (h j c) -> p h j c", h=2, j=4)
-                for j in range(4):
-                    nc.tensor.transpose(by_head[:, :, j, :], qs[(i, m)][:, P * j:P * (j + 1)], ident_hc)
+        def products(r, m):
+            prod[(r, m)] = abp.tile([P, 2, 512], F32, name="ab")
+            nc.vector.scalar_tensor_tensor(out=prod[(r, m)][:],
+                                           in0=acc[(r, m)][:].unsqueeze(1).to_broadcast([P, 2, 512]),
+                                           scalar=bias_of(r, m), in1=chan[:], op0=ALU.add, op1=ALU.mult)
 
-        def rope(i, tiles=(0, 1)):
-            if 0 in tiles:
-                ab[i] = abp.tile([P, 2, 2, 512], F32, name="ab")
-            for m in tiles:
-                tv = tb[(i, m)][:].rearrange("p (h c) -> p h c", h=2).unsqueeze(1).to_broadcast([P, 2, 2, 256])
-                tab_v = rope_t[:, m].rearrange("p e j r c -> p e (j r c)").unsqueeze(2).to_broadcast([P, 2, 2, 256])
-                nc.vector.tensor_tensor(out=ab[i][:, m].rearrange("p e (h c) -> p e h c", h=2), in0=tv,
-                                        in1=tab_v, op=ALU.mult)
+        def back(r, m):
+            bk = bank("O%d" % m)
+            for j in range(4):
+                cols = slice(P * j, P * (j + 1))
+                nc.tensor.matmul(bk[:, cols], lhsT=prod[(r, m)][:, 0, cols], rhs=ident[:], is_transpose=True,
+                                 start=True, stop=False)
+                nc.tensor.matmul(bk[:, cols], lhsT=prod[(r, m)][:, 1, cols], rhs=swap[:], is_transpose=True,
+                                 start=False, stop=True)
+            ob[(r, m)] = obp.tile([P, 512], F32, name="ob")
+            return bk
 
-        def add_store(i):
-            k, n = rounds[i]
-            head = 2 * (k % 4)
-            dst = outs[k // 4][n, head:head + 2].rearrange("h (p j) d -> p h (j d)", j=4)
-            ob = obp.tile([P, 2, 512], F32, name="ob")
-            a_v = ab[i][:, 0].rearrange("p e c -> p c e")
-            b_v = ab[i][:, 1].rearrange("p e c -> p c e")
-            o_v = ob[:].rearrange("p h (c e) -> p (h c) e", e=2)
-            if i < FIRST_VECTOR_ADD:
-                nc.gpsimd.tensor_tensor(out=o_v, in0=a_v, in1=b_v, op=ALU.add)
-                nc.sync.dma_start(out=dst, in_=ob[:])
-            else:
-                for h in range(2):
-                    cols = slice(256 * h, 256 * (h + 1))
-                    nc.vector.tensor_tensor(out=o_v[:, cols, :], in0=a_v[:, cols, :], in1=b_v[:, cols, :], op=ALU.add)
-                    nc.sync.dma_start(out=dst[:, h, :], in_=ob[:, h, :])
+        def finish(r, m, bk, eng):
+            copy_out(eng, ob[(r, m)][:], bk[:])
+            store(r, m)
 
-        w_in(0, 0, "IN0")
-        w_in(0, 1, "IN1")
-        for j in range(4):
-            x_in(0, j, "T%d%d" % (j // 2, j % 2))
-            if j == 0:
-                w_quant(0)
-            else:
-                x_quant(0, j - 1)
+        def store(r, m):
+            k, n = rounds[r]
+            nc.sync.dma_start(out=outs[k // 4][n, 2 * (k % 4) + m].rearrange("(p j) d -> p (j d)", j=4),
+                              in_=ob[(r, m)][:])
+
+        biased = {}
+
+        def bias_out(r, m):
+            biased[(r, m)] = qsp.tile([P, 512], F32, name="qs")
+            nc.scalar.activation(out=biased[(r, m)][:], in_=acc[(r, m)][:], func=ACT.Identity, bias=bias_of(r, m),
+                                 scale=1.0)
+
+        def back_plain(r, m):
+            bk = bank("O%d" % m)
+            for j in range(4):
+                cols = slice(P * j, P * (j + 1))
+                nc.tensor.transpose(bk[:, cols], biased[(r, m)][:, cols], ident[:])
+            return bk
+
+        def products_plain(r, m, bk):
+            prod[(r, m)] = abp.tile([P, 2, 512], F32, name="ab")
+            nc.vector.tensor_tensor(out=prod[(r, m)][:], in0=bk[:].unsqueeze(1).to_broadcast([P, 2, 512]),
+                                    in1=tok[:].rearrange("p a j h c -> p a (j h c)"), op=ALU.mult)
+
+        def add_plain(r, m, eng):
+            ob[(r, m)] = obp.tile([P, 512], F32, name="ob")
+            eng.tensor_tensor(out=ob[(r, m)][:].rearrange("p (c e) -> p c e", e=2),
+                              in0=prod[(r, m)][:, 0, :].rearrange("p (c e) -> p c e", e=2),
+                              in1=prod[(r, m)][:, 1, :].rearrange("p (c e) -> p c e", e=2)[:, :, ::-1], op=ALU.add)
+            store(r, m)
+
+        def bias_columns(tag):
+            nc.vector.tensor_copy(out=bf[:], in_=bz[:])
+            bk = bank(tag)
+            nc.tensor.transpose(bk[:, 0:P], bf[:], ident[:])
+            nc.scalar.copy(out=bias_sb[:], in_=bk[:, 0:16])
+
+        def sines():
+            nc.scalar.activation(out=tok[:, 0], in_=rc[:].unsqueeze(2).to_broadcast([P, 4, 2, 64]), func=ACT.Sin,
+                                 bias=half_pi[:, 0:1])
+            nc.scalar.activation(out=tok[:, 1], in_=rs[:].unsqueeze(2).to_broadcast([P, 4, 2, 64]), func=ACT.Sin)
+
+        def chan_table(a, tag, eng):
+            bk = bank(tag)
+            for j in range(4):
+                nc.tensor.transpose(bk[:, P * j:P * (j + 1)], tok[:, a, j].rearrange("p h c -> p (h c)"), ident[:])
+            copy_out(eng, chan[:, a, :], bk[:])
+
+        x_in(0, 0, "A00", S)
+        x_in(0, 1, "A01", V)
+        x_quant(0, 0)
+        w_in(0, 0, "IN0", S)
+        x_quant(0, 1)
+        w_in(0, 1, "IN1", V)
+        sines()
+        bias_columns("O0")
+        w_quant(0)
+        x_in(0, 2, "A10", S)
+        x_in(0, 3, "A11", V)
+        x_quant(0, 2)
         x_quant(0, 3)
-        nc.vector.tensor_scalar(out=gs[:], in0=r2[:], scalar1=math.pi, scalar2=-TWO_PI, op0=ALU.is_gt, op1=ALU.mult)
-        nc.vector.tensor_scalar(out=gc[:], in0=r2[:], scalar1=0.5 * math.pi, scalar2=-TWO_PI,
-                                op0=ALU.is_gt, op1=ALU.mult)
-        nc.vector.tensor_tensor(out=rs[:], in0=r2[:], in1=gs[:], op=ALU.add)
-        nc.vector.scalar_tensor_tensor(out=rc[:], in0=r2[:], scalar=0.5 * math.pi, in1=gc[:],
-                                       op0=ALU.add, op1=ALU.add)
-        bias_ps = bank("ACC1")
-        for m in range(2):
-            nc.tensor.transpose(bias_ps[:, P * m:P * (m + 1)], bf[:, m, :], ident[:])
-        nc.scalar.copy(out=bias_sb[:], in_=bias_ps[:, 0:256].rearrange("p (m r) -> p m r", m=2)[:, :, 0:8])
-        w_in(1, 0, "IN0")
-        w_in(1, 1, "IN1")
+        chan_table(0, "O0", S)
+        chan_table(1, "O1", V)
+        w_in(1, 0, "IN0", S)
+        w_in(1, 1, "IN1", S)
+        mx(0, 0)
+        mx(0, 1)
         w_quant(1)
-        for e in range(2):
-            rc_v = rc[:].rearrange("p j (c e) -> p e j c", e=2)[:, e].unsqueeze(2).to_broadcast([P, 4, 2, 32])
-            rs_v = rs[:].rearrange("p j (c e) -> p e j c", e=2)[:, e].unsqueeze(2).to_broadcast([P, 4, 2, 32])
-            nc.scalar.activation(out=rope_t[:, e, e], in_=rc_v, func=ACT.Sin)
-            nc.scalar.activation(out=rope_t[:, 1 - e, e], in_=rs_v, func=ACT.Sin, scale=(-1.0 if e == 0 else 1.0))
-        mx(0)
-        x_in(1, 0, "T10")
-        x_in(1, 1, "T11")
-        x_in(1, 2, "IN0")
-        x_in(1, 3, "IN1")
-        back(0)
-        x_quant(1, 0)
-        x_quant(1, 1)
-        rope(0, (0,))
-        x_quant(1, 2)
-        x_quant(1, 3)
-        rope(0, (1,))
-        add_store(0)
-
-        for r in range(1, LAST_DIRECT + 1):
-            mx(r)
-            w_in(r + 1, 0, "IN0")
-            w_in(r + 1, 1, "IN1")
-            back(r)
-            rope(r)
-            add_store(r)
-            w_quant(r + 1)
-        mx(LAST_DIRECT + 1)
-        for r in range(LAST_DIRECT + 2, N_ROUNDS):
-            mx(r)
-            back(r - 1)
-            rope(r - 1)
-            if r - 1 < FIRST_VECTOR_ADD:
-                add_store(r - 1)
-        back(N_ROUNDS - 1)
-        rope(N_ROUNDS - 1)
-        for r in range(FIRST_VECTOR_ADD, N_ROUNDS):
-            add_store(r)
+        products(0, 0)
+        products(0, 1)
+        x_in(1, 0, "IN0", S)
+        x_in(1, 1, "IN1", S)
+        for r in range(16):
+            if r == 0:
+                mx(1, 0)
+                mx(1, 1)
+                x_in(1, 2, "IN0", S)
+                x_in(1, 3, "IN1", S)
+            elif r + 1 < 16:
+                mx(r + 1, 0)
+                mx(r + 1, 1)
+            k = r // 2 + 2
+            if r % 2 == 1 and k < 8 or r == 0:
+                w_in(k, 0, "IN0", S)
+                w_in(k, 1, "IN1", S)
+            bks = [back(r, m) for m in range(2)]
+            if r == 0:
+                for j in range(4):
+                    x_quant(1, j)
+            if r + 1 < 16:
+                for m in range(2):
+                    products(r + 1, m)
+            for m in range(2):
+                finish(r, m, bks[m], S)
+            if r % 2 == 1 and k < 8 or r == 0:
+                w_quant(k)

@@ -264,49 +264,63 @@ def tile_l1regressionmoeactionhead_pa_kernel(tc, x, W_qa, b_qa, W_qt, b_qt, out_
 
         x_in(0, 0, "A00", S)
         x_in(0, 1, "A01", V)
-        x_quant(0, 0)
         w_in(0, 0, "IN0", S)
-        x_quant(0, 1)
         w_in(0, 1, "IN1", V)
-        sines()
+        x_quant(0, 0)
+        x_quant(0, 1)
+        x_in(0, 2, "A10", S)
+        x_in(0, 3, "A11", S)
         bias_columns("O0")
         w_quant(0)
-        x_in(0, 2, "A10", S)
-        x_in(0, 3, "A11", V)
         x_quant(0, 2)
         x_quant(0, 3)
-        chan_table(0, "O0", S)
-        chan_table(1, "O1", V)
-        w_in(1, 0, "IN0", S)
-        w_in(1, 1, "IN1", S)
-        mx(0, 0)
-        mx(0, 1)
+        w_in(1, 0, "IN0", V)
+        sines()
+        plain = lambda r, m: m == 1 or r == 0
+        bks = {}
+        for m in range(2):
+            mx(0, m)
+            bias_out(0, m)
+        w_in(1, 1, "IN1", V)
+        x_in(1, 0, "A10", S)
         w_quant(1)
-        products(0, 0)
-        products(0, 1)
-        x_in(1, 0, "IN0", S)
-        x_in(1, 1, "IN1", S)
-        for r in range(16):
-            if r == 0:
-                mx(1, 0)
-                mx(1, 1)
-                x_in(1, 2, "IN0", S)
-                x_in(1, 3, "IN1", S)
-            elif r + 1 < 16:
-                mx(r + 1, 0)
-                mx(r + 1, 1)
-            k = r // 2 + 2
-            if r % 2 == 1 and k < 8 or r == 0:
-                w_in(k, 0, "IN0", S)
-                w_in(k, 1, "IN1", S)
-            bks = [back(r, m) for m in range(2)]
-            if r == 0:
-                for j in range(4):
-                    x_quant(1, j)
-            if r + 1 < 16:
-                for m in range(2):
-                    products(r + 1, m)
+        for m in range(2):
+            bks[m] = back_plain(0, m)
+            products_plain(0, m, bks[m])
+            add_plain(0, m, G)
+        x_in(1, 1, "IN0", S)
+        x_quant(1, 0)
+        mx(1, 0)
+        mx(1, 1)
+        bias_out(1, 1)
+        x_in(1, 2, "IN1", V)
+        x_in(1, 3, "IN0", S)
+        chan_table(0, "A00", S)
+        chan_table(1, "O0", V)
+        x_quant(1, 1)
+        x_quant(1, 2)
+        products(1, 0)
+        x_quant(1, 3)
+        w_in(2, 0, "IN1", S)
+        for r in range(2, 17):
             for m in range(2):
-                finish(r, m, bks[m], S)
-            if r % 2 == 1 and k < 8 or r == 0:
-                w_quant(k)
+                if r < 16:
+                    mx(r, m)
+                    if plain(r, m):
+                        bias_out(r, m)
+            for m in range(2):
+                bks[m] = back_plain(r - 1, m) if plain(r - 1, m) else back(r - 1, m)
+                if not plain(r - 1, m):
+                    finish(r - 1, m, bks[m], S)
+            k = (r + 3) // 2 if r % 2 else (r + 2) // 2
+            if k < 8:
+                w_in(k, (r + 1) % 2, "IN%d" % (r % 2), S)
+            for m in range(2):
+                if r < 16 and not plain(r, m):
+                    products(r, m)
+            if r % 2 and r // 2 + 1 < 8:
+                w_quant(r // 2 + 1)
+            for m in range(2):
+                if plain(r - 1, m):
+                    products_plain(r - 1, m, bks[m])
+                    add_plain(r - 1, m, G)

@@ -32,6 +32,7 @@ def tile_l1regressionmoeactionhead_pa_kernel(tc, x, W_qa, b_qa, W_qt, b_qt, out_
         wgp = ctx.enter_context(tc.tile_pool(name="wgp", bufs=3))
         abp = ctx.enter_context(tc.tile_pool(name="abp", bufs=6))
         qsp = ctx.enter_context(tc.tile_pool(name="qsp", bufs=3))
+        srt = ctx.enter_context(tc.tile_pool(name="srt", bufs=3))
         obp = ctx.enter_context(tc.tile_pool(name="obp", bufs=6))
         psum = ctx.enter_context(tc.psum_pool(name="psum", bufs=1))
         ctx.enter_context(tc.manual_schedule())
@@ -91,11 +92,12 @@ def tile_l1regressionmoeactionhead_pa_kernel(tc, x, W_qa, b_qa, W_qt, b_qt, out_
             load_w(0, m)
         for j in range(2, 4):
             load_x(0, j)
-        for m in range(2):
-            load_w(1, m)
+        for k in range(1, 3):
+            for m in range(2):
+                load_w(k, m)
         for j in range(4):
             load_x(1, j)
-        for k in range(2, 8):
+        for k in range(3, 8):
             for m in range(2):
                 load_w(k, m)
 
@@ -140,6 +142,22 @@ def tile_l1regressionmoeactionhead_pa_kernel(tc, x, W_qa, b_qa, W_qt, b_qt, out_
                 nc.tensor.transpose(bk[:, P * q:P * (q + 1)], src32[:, first:first + 2 * P - 1:2], ident[:])
             return bk[:].rearrange("p (g u r) -> p g r u", g=2, u=2)
 
+        sorted_w = {}
+
+        def sort_words(k, m, eng):
+            sorted_w[(k, m)] = srt.tile([P, 512], F32, name="srt")
+            copy_out(eng, sorted_w[(k, m)][:].rearrange("p (g u r) -> p g u r", g=2, u=2),
+                     w_sb[k][m][:].bitcast(F32).rearrange("p (g r u) -> p g u r", g=2, u=2))
+
+        def sorted_in(k, m, tag, eng):
+            if m == 0:
+                wg[k] = wgp.tile([P, 2048], BF16, name="wg", align_bytes=64)
+            bk = bank(tag)
+            for q in range(4):
+                nc.tensor.transpose(bk[:, P * q:P * (q + 1)], sorted_w[(k, m)][:, P * q:P * (q + 1)], ident[:])
+            dst = wg[k][:].bitcast(F32)[:, 512 * m:512 * (m + 1)].rearrange("p (g r u) -> p g r u", g=2, u=2)
+            copy_out(eng, dst, bk[:].rearrange("p (g u r) -> p g r u", g=2, u=2))
+
         def copy_out(eng, out, in_):
             if eng is nc.scalar:
                 nc.scalar.copy(out=out, in_=in_)
@@ -173,7 +191,7 @@ def tile_l1regressionmoeactionhead_pa_kernel(tc, x, W_qa, b_qa, W_qt, b_qt, out_
                 nc.vector.quantize_mx(out=xcodes[n][:, c0:c0 + P].bitcast(FP8X4), scales=xscales[n][:, c0:c0 + P],
                                       in_=xg[n][j][:, 512 * g:512 * (g + 1)])
 
-        rounds = [(0, 0), (1, 0), (0, 1), (1, 1)] + [(k, n) for k in range(2, 8) for n in range(2)]
+        rounds = [(k, n) for n in range(2) for k in range(3)] + [(k, n) for k in range(3, 8) for n in range(2)]
         acc = {}
         prod = {}
         ob = {}
@@ -245,8 +263,10 @@ def tile_l1regressionmoeactionhead_pa_kernel(tc, x, W_qa, b_qa, W_qt, b_qt, out_
                               in1=prod[(r, m)][:, 1, :].rearrange("p (c e) -> p c e", e=2)[:, :, ::-1], op=ALU.add)
             store(r, m)
 
-        def bias_columns(tag):
+        def bias_cast():
             nc.vector.tensor_copy(out=bf[:], in_=bz[:])
+
+        def bias_columns(tag):
             bk = bank(tag)
             nc.tensor.transpose(bk[:, 0:P], bf[:], ident[:])
             nc.scalar.copy(out=bias_sb[:], in_=bk[:, 0:16])
@@ -262,6 +282,7 @@ def tile_l1regressionmoeactionhead_pa_kernel(tc, x, W_qa, b_qa, W_qt, b_qt, out_
                 nc.tensor.transpose(bk[:, P * j:P * (j + 1)], tok[:, a, j].rearrange("p h c -> p (h c)"), ident[:])
             copy_out(eng, chan[:, a, :], bk[:])
 
+        plain = lambda r, m: m == 1 or r <= 2
         x_in(0, 0, "A00", S)
         x_in(0, 1, "A01", V)
         w_in(0, 0, "IN0", S)
@@ -270,39 +291,47 @@ def tile_l1regressionmoeactionhead_pa_kernel(tc, x, W_qa, b_qa, W_qt, b_qt, out_
         x_quant(0, 1)
         x_in(0, 2, "A10", S)
         x_in(0, 3, "A11", S)
-        bias_columns("O0")
+        bias_cast()
         w_quant(0)
         x_quant(0, 2)
         x_quant(0, 3)
         w_in(1, 0, "IN0", V)
+        w_in(1, 1, "IN1", V)
+        w_quant(1)
+        bias_columns("O0")
         sines()
-        plain = lambda r, m: m == 1 or r == 0
         bks = {}
         for m in range(2):
             mx(0, m)
             bias_out(0, m)
-        w_in(1, 1, "IN1", V)
-        x_in(1, 0, "A10", S)
-        w_quant(1)
+        w_in(2, 0, "IN0", S)
         for m in range(2):
             bks[m] = back_plain(0, m)
             products_plain(0, m, bks[m])
             add_plain(0, m, G)
-        x_in(1, 1, "IN0", S)
-        x_quant(1, 0)
-        mx(1, 0)
-        mx(1, 1)
-        bias_out(1, 1)
-        x_in(1, 2, "IN1", V)
-        x_in(1, 3, "IN0", S)
-        chan_table(0, "A00", S)
-        chan_table(1, "O0", V)
-        x_quant(1, 1)
+        w_in(2, 1, "IN1", S)
+        w_quant(2)
+        for m in range(2):
+            mx(1, m)
+            bias_out(1, m)
+        x_in(1, 0, "IN0", S)
+        x_in(1, 1, "IN1", S)
+        for m in range(2):
+            bks[m] = back_plain(1, m)
+            products_plain(1, m, bks[m])
+            add_plain(1, m, G)
+            x_quant(1, m)
+        for m in range(2):
+            mx(2, m)
+            bias_out(2, m)
+        x_in(1, 2, "IN0", S)
+        x_in(1, 3, "IN1", S)
         x_quant(1, 2)
-        products(1, 0)
         x_quant(1, 3)
-        w_in(2, 0, "IN1", S)
-        for r in range(2, 17):
+        chan_table(0, "A00", S)
+        chan_table(1, "A01", S)
+        sort_words(3, 0, S)
+        for r in range(3, 17):
             for m in range(2):
                 if r < 16:
                     mx(r, m)
@@ -312,15 +341,17 @@ def tile_l1regressionmoeactionhead_pa_kernel(tc, x, W_qa, b_qa, W_qt, b_qt, out_
                 bks[m] = back_plain(r - 1, m) if plain(r - 1, m) else back(r - 1, m)
                 if not plain(r - 1, m):
                     finish(r - 1, m, bks[m], S)
-            k = (r + 3) // 2 if r % 2 else (r + 2) // 2
-            if k < 8:
-                w_in(k, (r + 1) % 2, "IN%d" % (r % 2), S)
+            k = (r + 3) // 2
+            if 3 <= k < 8:
+                sorted_in(k, (r + 1) % 2, "IN%d" % (r % 2), S)
+            if 3 <= (r + 4) // 2 < 8:
+                sort_words((r + 4) // 2, r % 2, S)
             for m in range(2):
                 if r < 16 and not plain(r, m):
                     products(r, m)
-            if r % 2 and r // 2 + 1 < 8:
-                w_quant(r // 2 + 1)
+            if r % 2 and r > 3 and (r + 1) // 2 < 8:
+                w_quant((r + 1) // 2)
             for m in range(2):
                 if plain(r - 1, m):
                     products_plain(r - 1, m, bks[m])
-                    add_plain(r - 1, m, G)
+                    add_plain(r - 1, m, V if r == 16 else G)

@@ -30,10 +30,9 @@ def tile_l1regressionmoeactionhead_pa_kernel(tc, x, W_qa, b_qa, W_qt, b_qt, out_
     with ExitStack() as ctx:
         keep = ctx.enter_context(tc.tile_pool(name="keep", bufs=1))
         wgp = ctx.enter_context(tc.tile_pool(name="wgp", bufs=3))
-        abp = ctx.enter_context(tc.tile_pool(name="abp", bufs=6))
-        qsp = ctx.enter_context(tc.tile_pool(name="qsp", bufs=3))
-        srt = ctx.enter_context(tc.tile_pool(name="srt", bufs=3))
-        obp = ctx.enter_context(tc.tile_pool(name="obp", bufs=6))
+        abp = ctx.enter_context(tc.tile_pool(name="abp", bufs=8))
+        qsp = ctx.enter_context(tc.tile_pool(name="qsp", bufs=5))
+        obp = ctx.enter_context(tc.tile_pool(name="obp", bufs=10))
         psum = ctx.enter_context(tc.psum_pool(name="psum", bufs=1))
         ctx.enter_context(tc.manual_schedule())
 
@@ -92,12 +91,12 @@ def tile_l1regressionmoeactionhead_pa_kernel(tc, x, W_qa, b_qa, W_qt, b_qt, out_
             load_w(0, m)
         for j in range(2, 4):
             load_x(0, j)
-        for k in range(1, 3):
+        for k in range(1, 4):
             for m in range(2):
                 load_w(k, m)
         for j in range(4):
             load_x(1, j)
-        for k in range(3, 8):
+        for k in range(4, 8):
             for m in range(2):
                 load_w(k, m)
 
@@ -142,22 +141,6 @@ def tile_l1regressionmoeactionhead_pa_kernel(tc, x, W_qa, b_qa, W_qt, b_qt, out_
                 nc.tensor.transpose(bk[:, P * q:P * (q + 1)], src32[:, first:first + 2 * P - 1:2], ident[:])
             return bk[:].rearrange("p (g u r) -> p g r u", g=2, u=2)
 
-        sorted_w = {}
-
-        def sort_words(k, m, eng):
-            sorted_w[(k, m)] = srt.tile([P, 512], F32, name="srt")
-            copy_out(eng, sorted_w[(k, m)][:].rearrange("p (g u r) -> p g u r", g=2, u=2),
-                     w_sb[k][m][:].bitcast(F32).rearrange("p (g r u) -> p g u r", g=2, u=2))
-
-        def sorted_in(k, m, tag, eng):
-            if m == 0:
-                wg[k] = wgp.tile([P, 2048], BF16, name="wg", align_bytes=64)
-            bk = bank(tag)
-            for q in range(4):
-                nc.tensor.transpose(bk[:, P * q:P * (q + 1)], sorted_w[(k, m)][:, P * q:P * (q + 1)], ident[:])
-            dst = wg[k][:].bitcast(F32)[:, 512 * m:512 * (m + 1)].rearrange("p (g r u) -> p g r u", g=2, u=2)
-            copy_out(eng, dst, bk[:].rearrange("p (g u r) -> p g r u", g=2, u=2))
-
         def copy_out(eng, out, in_):
             if eng is nc.scalar:
                 nc.scalar.copy(out=out, in_=in_)
@@ -191,14 +174,14 @@ def tile_l1regressionmoeactionhead_pa_kernel(tc, x, W_qa, b_qa, W_qt, b_qt, out_
                 nc.vector.quantize_mx(out=xcodes[n][:, c0:c0 + P].bitcast(FP8X4), scales=xscales[n][:, c0:c0 + P],
                                       in_=xg[n][j][:, 512 * g:512 * (g + 1)])
 
-        rounds = [(k, n) for n in range(2) for k in range(3)] + [(k, n) for k in range(3, 8) for n in range(2)]
+        rounds = [(k, n) for n in range(2) for k in range(4)] + [(k, n) for k in range(4, 8) for n in range(2)]
         acc = {}
         prod = {}
         ob = {}
 
         def mx(r, m):
             k, n = rounds[r]
-            acc[(r, m)] = bank("A%d%d" % (r % 2, m))
+            acc[(r, m)] = bank("A%d" % m)
             for g in range(2):
                 s0 = P * (2 * m + g)
                 nc.tensor.matmul_mx(out=acc[(r, m)][:],
@@ -218,7 +201,7 @@ def tile_l1regressionmoeactionhead_pa_kernel(tc, x, W_qa, b_qa, W_qt, b_qt, out_
                                            scalar=bias_of(r, m), in1=chan[:], op0=ALU.add, op1=ALU.mult)
 
         def back(r, m):
-            bk = bank("O%d" % m)
+            bk = bank("O%d%d" % (r % 2, m))
             for j in range(4):
                 cols = slice(P * j, P * (j + 1))
                 nc.tensor.matmul(bk[:, cols], lhsT=prod[(r, m)][:, 0, cols], rhs=ident[:], is_transpose=True,
@@ -245,7 +228,7 @@ def tile_l1regressionmoeactionhead_pa_kernel(tc, x, W_qa, b_qa, W_qt, b_qt, out_
                                  scale=1.0)
 
         def back_plain(r, m):
-            bk = bank("O%d" % m)
+            bk = bank("O%d%d" % (r % 2, m))
             for j in range(4):
                 cols = slice(P * j, P * (j + 1))
                 nc.tensor.transpose(bk[:, cols], biased[(r, m)][:, cols], ident[:])
@@ -282,15 +265,14 @@ def tile_l1regressionmoeactionhead_pa_kernel(tc, x, W_qa, b_qa, W_qt, b_qt, out_
                 nc.tensor.transpose(bk[:, P * j:P * (j + 1)], tok[:, a, j].rearrange("p h c -> p (h c)"), ident[:])
             copy_out(eng, chan[:, a, :], bk[:])
 
-        plain = lambda r, m: m == 1 or r <= 2
-        x_in(0, 0, "A00", S)
-        x_in(0, 1, "A01", V)
+        x_in(0, 0, "O00", S)
+        x_in(0, 1, "O01", V)
         w_in(0, 0, "IN0", S)
         w_in(0, 1, "IN1", V)
         x_quant(0, 0)
         x_quant(0, 1)
-        x_in(0, 2, "A10", S)
-        x_in(0, 3, "A11", S)
+        x_in(0, 2, "O10", S)
+        x_in(0, 3, "O11", S)
         bias_cast()
         w_quant(0)
         x_quant(0, 2)
@@ -298,60 +280,59 @@ def tile_l1regressionmoeactionhead_pa_kernel(tc, x, W_qa, b_qa, W_qt, b_qt, out_
         w_in(1, 0, "IN0", V)
         w_in(1, 1, "IN1", V)
         w_quant(1)
-        bias_columns("O0")
+        bias_columns("A0")
         sines()
+        units = [("w", 2, 0), ("w", 2, 1), ("w", 3, 0), ("w", 3, 1)] + [("x", 1, j) for j in range(4)]
+        units = units + [("w", k, m) for k in range(4, 8) for m in range(2)]
+        done = []
         bks = {}
-        for m in range(2):
-            mx(0, m)
-            bias_out(0, m)
-        w_in(2, 0, "IN0", S)
-        for m in range(2):
-            bks[m] = back_plain(0, m)
-            products_plain(0, m, bks[m])
-            add_plain(0, m, G)
-        w_in(2, 1, "IN1", S)
-        w_quant(2)
-        for m in range(2):
-            mx(1, m)
-            bias_out(1, m)
-        x_in(1, 0, "IN0", S)
-        x_in(1, 1, "IN1", S)
-        for m in range(2):
-            bks[m] = back_plain(1, m)
-            products_plain(1, m, bks[m])
-            add_plain(1, m, G)
-            x_quant(1, m)
-        for m in range(2):
-            mx(2, m)
-            bias_out(2, m)
-        x_in(1, 2, "IN0", S)
-        x_in(1, 3, "IN1", S)
-        x_quant(1, 2)
-        x_quant(1, 3)
-        chan_table(0, "A00", S)
-        chan_table(1, "A01", S)
-        sort_words(3, 0, S)
-        for r in range(3, 17):
+
+        def unit(count=1):
+            for i in range(count):
+                if len(done) < len(units):
+                    kind, a, b = units[len(done)]
+                    if kind == "w":
+                        w_in(a, b, "IN%d" % (len(done) % 2), S)
+                    else:
+                        x_in(a, b, "IN%d" % (len(done) % 2), S)
+                    done.append(0)
+
+        def rotate(r, m):
+            products_plain(r, m, bks[(r, m)])
+            add_plain(r, m, V if r == 15 and m == 1 else G)
+
+        for r in range(16):
             for m in range(2):
-                if r < 16:
-                    mx(r, m)
-                    if plain(r, m):
-                        bias_out(r, m)
-            for m in range(2):
-                bks[m] = back_plain(r - 1, m) if plain(r - 1, m) else back(r - 1, m)
-                if not plain(r - 1, m):
-                    finish(r - 1, m, bks[m], S)
-            k = (r + 3) // 2
-            if 3 <= k < 8:
-                sorted_in(k, (r + 1) % 2, "IN%d" % (r % 2), S)
-            if 3 <= (r + 4) // 2 < 8:
-                sort_words((r + 4) // 2, r % 2, S)
-            for m in range(2):
-                if r < 16 and not plain(r, m):
-                    products(r, m)
-            if r % 2 and r > 3 and (r + 1) // 2 < 8:
-                w_quant((r + 1) // 2)
-            for m in range(2):
-                if plain(r - 1, m):
-                    products_plain(r - 1, m, bks[m])
-                    add_plain(r - 1, m, V if r == 16 else G)
+                mx(r, m)
+                bias_out(r, m)
+            if r < 4:
+                unit(1)
+                bks[(r, 0)] = back_plain(r, 0)
+                if r == 3:
+                    x_quant(1, 2)
+                rotate(r, 0)
+                if r == 2:
+                    x_quant(1, 0)
+                if r == 3:
+                    x_quant(1, 3)
+                unit(2 if r == 2 else 1)
+                bks[(r, 1)] = back_plain(r, 1)
+                rotate(r, 1)
+                if r < 2:
+                    w_quant(2 + r)
+                if r == 2:
+                    x_quant(1, 1)
+            else:
+                if r > 4:
+                    for m in range(2):
+                        bks[(r - 1, m)] = back_plain(r - 1, m)
+                unit(1)
+                if r > 4:
+                    rotate(r - 1, 0)
+                if r in (5, 7, 9, 11):
+                    w_quant((r + 3) // 2)
+                if r > 4:
+                    rotate(r - 1, 1)
+        for m in range(2):
+            bks[(15, m)] = back_plain(15, m)
+            rotate(15, m)

@@ -32,6 +32,7 @@ def tile_l1regressionmoeactionhead_pa_kernel(tc, x, W_qa, b_qa, W_qt, b_qt, out_
         wgp = ctx.enter_context(tc.tile_pool(name="wgp", bufs=3))
         abp = ctx.enter_context(tc.tile_pool(name="abp", bufs=8))
         qsp = ctx.enter_context(tc.tile_pool(name="qsp", bufs=5))
+        srt = ctx.enter_context(tc.tile_pool(name="srt", bufs=3))
         obp = ctx.enter_context(tc.tile_pool(name="obp", bufs=10))
         psum = ctx.enter_context(tc.psum_pool(name="psum", bufs=1))
         ctx.enter_context(tc.manual_schedule())
@@ -134,12 +135,22 @@ def tile_l1regressionmoeactionhead_pa_kernel(tc, x, W_qa, b_qa, W_qt, b_qt, out_
         nc.gpsimd.tensor_tensor(out=rs_v[:, :, :, 0], in0=r2_v[:, :, :, 1], in1=gs_v[:, :, :, 1], op=ALU.subtract)
         nc.gpsimd.tensor_tensor(out=rs_v[:, :, :, 1], in0=gs_v[:, :, :, 0], in1=r2_v[:, :, :, 0], op=ALU.subtract)
 
-        def words_in(src32, tag):
+        def words_in(src32, tag, key=None):
             bk = bank(tag)
             for q in range(4):
                 first = 2 * P * (q // 2) + q % 2
-                nc.tensor.transpose(bk[:, P * q:P * (q + 1)], src32[:, first:first + 2 * P - 1:2], ident[:])
+                words = src32[:, first:first + 2 * P - 1:2]
+                if key in ordered:
+                    words = ordered[key][:, P * q:P * (q + 1)]
+                nc.tensor.transpose(bk[:, P * q:P * (q + 1)], words, ident[:])
             return bk[:].rearrange("p (g u r) -> p g r u", g=2, u=2)
+
+        ordered = {}
+
+        def order_words(key, src, eng):
+            ordered[key] = srt.tile([P, 512], F32, name="srt")
+            copy_out(eng, ordered[key][:].rearrange("p (g u r) -> p g u r", g=2, u=2),
+                     src.bitcast(F32).rearrange("p (g r u) -> p g u r", g=2, u=2))
 
         def copy_out(eng, out, in_):
             if eng is nc.scalar:
@@ -152,7 +163,7 @@ def tile_l1regressionmoeactionhead_pa_kernel(tc, x, W_qa, b_qa, W_qt, b_qt, out_
         def w_in(k, m, tag, eng):
             if m == 0:
                 wg[k] = wgp.tile([P, 2048], BF16, name="wg", align_bytes=64)
-            src = words_in(w_sb[k][m][:].bitcast(F32), tag)
+            src = words_in(w_sb[k][m][:].bitcast(F32), tag, ("w", k, m))
             dst = wg[k][:].bitcast(F32)[:, 512 * m:512 * (m + 1)].rearrange("p (g r u) -> p g r u", g=2, u=2)
             copy_out(eng, dst, src)
 
@@ -165,7 +176,7 @@ def tile_l1regressionmoeactionhead_pa_kernel(tc, x, W_qa, b_qa, W_qt, b_qt, out_
                                   in_=wg[k][:, 4 * c0:4 * (c0 + 256)])
 
         def x_in(n, j, tag, eng):
-            src = words_in(x_sb[n][j][:].bitcast(F32), tag)
+            src = words_in(x_sb[n][j][:].bitcast(F32), tag, ("x", n, j))
             copy_out(eng, xg[n][j][:].bitcast(F32).rearrange("p (g c u) -> p g c u", g=2, u=2), src)
 
         def x_quant(n, j):
@@ -254,10 +265,12 @@ def tile_l1regressionmoeactionhead_pa_kernel(tc, x, W_qa, b_qa, W_qt, b_qt, out_
             nc.tensor.transpose(bk[:, 0:P], bf[:], ident[:])
             nc.scalar.copy(out=bias_sb[:], in_=bk[:, 0:16])
 
-        def sines():
-            nc.scalar.activation(out=tok[:, 0], in_=rc[:].unsqueeze(2).to_broadcast([P, 4, 2, 64]), func=ACT.Sin,
-                                 bias=half_pi[:, 0:1])
-            nc.scalar.activation(out=tok[:, 1], in_=rs[:].unsqueeze(2).to_broadcast([P, 4, 2, 64]), func=ACT.Sin)
+        def sine_table(a):
+            if a == 0:
+                nc.scalar.activation(out=tok[:, 0], in_=rc[:].unsqueeze(2).to_broadcast([P, 4, 2, 64]), func=ACT.Sin,
+                                     bias=half_pi[:, 0:1])
+            else:
+                nc.scalar.activation(out=tok[:, 1], in_=rs[:].unsqueeze(2).to_broadcast([P, 4, 2, 64]), func=ACT.Sin)
 
         def chan_table(a, tag, eng):
             bk = bank(tag)
@@ -266,73 +279,87 @@ def tile_l1regressionmoeactionhead_pa_kernel(tc, x, W_qa, b_qa, W_qt, b_qt, out_
             copy_out(eng, chan[:, a, :], bk[:])
 
         x_in(0, 0, "O00", S)
+        sine_table(0)
         x_in(0, 1, "O01", V)
-        w_in(0, 0, "IN0", S)
-        w_in(0, 1, "IN1", V)
         x_quant(0, 0)
         x_quant(0, 1)
+        w_in(0, 0, "IN0", S)
+        w_in(0, 1, "IN1", V)
         x_in(0, 2, "O10", S)
-        x_in(0, 3, "O11", S)
         bias_cast()
         w_quant(0)
+        x_in(0, 3, "O11", S)
+        sine_table(1)
         x_quant(0, 2)
         x_quant(0, 3)
         w_in(1, 0, "IN0", V)
         w_in(1, 1, "IN1", V)
         w_quant(1)
-        bias_columns("A0")
-        sines()
+        bias_columns("A1")
         units = [("w", 2, 0), ("w", 2, 1), ("w", 3, 0), ("w", 3, 1)] + [("x", 1, j) for j in range(4)]
         units = units + [("w", k, m) for k in range(4, 8) for m in range(2)]
         done = []
         bks = {}
 
+        def order(i, eng):
+            if i < len(units):
+                what, a, b = units[i]
+                order_words(units[i], w_sb[a][b][:] if what == "w" else x_sb[a][b][:], eng)
+
         def unit(count=1):
             for i in range(count):
                 if len(done) < len(units):
-                    kind, a, b = units[len(done)]
-                    if kind == "w":
+                    what, a, b = units[len(done)]
+                    if what == "w":
                         w_in(a, b, "IN%d" % (len(done) % 2), S)
                     else:
                         x_in(a, b, "IN%d" % (len(done) % 2), S)
                     done.append(0)
 
+        def turn(r, m):
+            bks[(r, m)] = back_plain(r, m)
+
         def rotate(r, m):
             products_plain(r, m, bks[(r, m)])
-            add_plain(r, m, V if r == 15 and m == 1 else G)
+            add_plain(r, m, V if r == 15 and m == 1 or r == 14 and m == 1 else G)
 
+        LAG = 11
         for r in range(16):
             for m in range(2):
                 mx(r, m)
                 bias_out(r, m)
-            if r < 4:
+            if r < LAG:
                 unit(1)
-                bks[(r, 0)] = back_plain(r, 0)
+                turn(r, 0)
                 if r == 3:
                     x_quant(1, 2)
+                    x_quant(1, 3)
                 rotate(r, 0)
                 if r == 2:
                     x_quant(1, 0)
-                if r == 3:
-                    x_quant(1, 3)
-                unit(2 if r == 2 else 1)
-                bks[(r, 1)] = back_plain(r, 1)
+                unit(0 if r > 3 else 2 if r == 2 else 1)
+                turn(r, 1)
                 rotate(r, 1)
                 if r < 2:
                     w_quant(2 + r)
                 if r == 2:
                     x_quant(1, 1)
+                if r in (5, 7, 9, 11):
+                    w_quant((r + 3) // 2)
+                if r >= 2:
+                    order(6 + r, S)
             else:
-                if r > 4:
+                if r > LAG:
                     for m in range(2):
-                        bks[(r - 1, m)] = back_plain(r - 1, m)
+                        turn(r - 1, m)
                 unit(1)
-                if r > 4:
+                order(r + 6, S)
+                if r > LAG:
                     rotate(r - 1, 0)
                 if r in (5, 7, 9, 11):
                     w_quant((r + 3) // 2)
-                if r > 4:
+                if r > LAG:
                     rotate(r - 1, 1)
         for m in range(2):
-            bks[(15, m)] = back_plain(15, m)
+            turn(15, m)
             rotate(15, m)

import math
from contextlib import ExitStack

import concourse.mybir as mybir
from concourse.masks import make_identity

F32 = mybir.dt.float32
BF16 = mybir.dt.bfloat16
I32 = mybir.dt.int32
U32 = mybir.dt.uint32
U8 = mybir.dt.uint8
FP8X4 = mybir.dt.float8_e4m3fn_x4
ALU = mybir.AluOpType
ACT = mybir.ActivationFunctionType

P = 128
FLOPS = 2 * 1024 * 1024 * 2048

TWO_PI = 2.0 * math.pi
C1 = 6.283203125
C2 = TWO_PI - C1
RATIO = 10000.0 ** (-1.0 / 64.0)


def tile_l1regressionmoeactionhead_pa_kernel(tc, x, W_qa, b_qa, W_qt, b_qt, out_0, out_1):
    nc = tc.nc
    weights = [W_qa, W_qt]
    outs = [out_0, out_1]
    V, S, G = nc.vector, nc.scalar, nc.gpsimd
    with ExitStack() as ctx:
        keep = ctx.enter_context(tc.tile_pool(name="keep", bufs=1))
        wgp = ctx.enter_context(tc.tile_pool(name="wgp", bufs=3))
        abp = ctx.enter_context(tc.tile_pool(name="abp", bufs=8))
        qsp = ctx.enter_context(tc.tile_pool(name="qsp", bufs=5))
        srt = ctx.enter_context(tc.tile_pool(name="srt", bufs=3))
        obp = ctx.enter_context(tc.tile_pool(name="obp", bufs=10))
        psum = ctx.enter_context(tc.psum_pool(name="psum", bufs=1))
        ctx.enter_context(tc.manual_schedule())

        def bank(tag):
            return psum.tile([P, 512], F32, name="bk" + tag, tag=tag)

        ident = keep.tile([P, P], F32, name="ident")
        swap = keep.tile([P, P], F32, name="swap")
        x_sb = [[keep.tile([P, 1024], BF16, name="x%d%d" % (n, j)) for j in range(4)] for n in range(2)]
        w_sb = [[keep.tile([P, 1024], BF16, name="w%d%d" % (k, m)) for m in range(2)] for k in range(8)]
        xg = [[keep.tile([P, 1024], BF16, name="xg%d%d" % (n, j), align_bytes=64) for j in range(4)] for n in range(2)]
        xcodes = [keep.tile([P, 1024], U32, name="xc%d" % n, align_bytes=64) for n in range(2)]
        xscales = [keep.tile([P, 1024], U8, name="xs%d" % n, align_bytes=64) for n in range(2)]
        wcodes = [keep.tile([P, 512], U32, name="wc%d" % k, align_bytes=64) for k in range(8)]
        wscales = [keep.tile([P, 512], U8, name="ws%d" % k, align_bytes=64) for k in range(8)]
        dm0 = keep.tile([P, 1], F32, name="dm0")
        dm1 = keep.tile([P, 1], F32, name="dm1")
        half_pi = keep.tile([P, 1], F32, name="half_pi")
        bz = keep.tile([P, P], BF16, name="bz")
        bf = keep.tile([P, P], F32, name="bf")
        bias_sb = keep.tile([P, 16], F32, name="bias_sb")
        freq = keep.tile([P, 64], F32, name="freq")
        t_i = keep.tile([P, 4], I32, name="t_i")
        t_f = keep.tile([P, 4], F32, name="t_f")
        ang = keep.tile([P, 4, 64], F32, name="ang")
        k_i = keep.tile([P, 4, 64], I32, name="k_i")
        k_f = keep.tile([P, 4, 64], F32, name="k_f")
        r1 = keep.tile([P, 4, 64], F32, name="r1")
        r2 = keep.tile([P, 4, 64], F32, name="r2")
        gs = keep.tile([P, 4, 64], F32, name="gs")
        gc = keep.tile([P, 4, 64], F32, name="gc")
        rs = keep.tile([P, 4, 64], F32, name="rs")
        rc = keep.tile([P, 4, 64], F32, name="rc")
        tok = keep.tile([P, 2, 4, 2, 64], F32, name="tok")
        chan = keep.tile([P, 2, 512], F32, name="chan")

        make_identity(nc, ident[:])
        nc.gpsimd.iota(t_i[:], pattern=[[1, 4]], base=0, channel_multiplier=4)
        nc.vector.memset(bz[:], 0.0)
        nc.vector.memset(dm0[:], 0.0)
        nc.vector.memset(freq[:, 0:1], 1.0)

        nc.scalar.dma_start(out=bz[0:8, :], in_=b_qa.rearrange("(r c) -> r c", c=P))
        nc.scalar.dma_start(out=bz[8:16, :], in_=b_qt.rearrange("(r c) -> r c", c=P))

        def load_w(k, m):
            row0 = 256 * (k % 4) + P * m
            nc.sync.dma_start(out=w_sb[k][m][:], in_=weights[k // 4][row0:row0 + P, :])

        def load_x(n, j):
            nc.sync.dma_start(out=x_sb[n][j][:], in_=x[n].rearrange("(p j) k -> p j k", j=4)[:, j, :])

        for j in range(2):
            load_x(0, j)
        for m in range(2):
            load_w(0, m)
        for j in range(2, 4):
            load_x(0, j)
        for k in range(1, 4):
            for m in range(2):
                load_w(k, m)
        for j in range(4):
            load_x(1, j)
        for k in range(4, 8):
            for m in range(2):
                load_w(k, m)

        nc.scalar.activation(out=dm1[:], in_=dm0[:], func=ACT.Sin)

        swap_v = swap[:].rearrange("p (c e) -> p c e", e=2)
        ident_v = ident[:].rearrange("p (c e) -> p c e", e=2)
        for e in range(2):
            nc.gpsimd.tensor_copy(out=swap_v[:, :, e], in_=ident_v[:, :, 1 - e])

        for c in range(1, 4):
            nc.vector.tensor_scalar(out=freq[:, c:c + 1], in0=freq[:, 0:1], scalar1=RATIO ** c,
                                    scalar2=None, op0=ALU.mult)
        for a in range(1, 4):
            nc.vector.tensor_scalar(out=freq[:, 4 * a:4 * a + 4], in0=freq[:, 0:4], scalar1=RATIO ** (4 * a),
                                    scalar2=None, op0=ALU.mult)
        nc.vector.tensor_scalar(out=half_pi[:], in0=freq[:, 0:1], scalar1=0.5 * math.pi, scalar2=None, op0=ALU.mult)
        for a in range(1, 4):
            nc.vector.tensor_scalar(out=freq[:, 16 * a:16 * a + 16], in0=freq[:, 0:16], scalar1=RATIO ** (16 * a),
                                    scalar2=None, op0=ALU.mult)
        nc.vector.tensor_copy(out=t_f[:], in_=t_i[:])
        nc.vector.tensor_tensor(out=ang[:], in0=freq[:].unsqueeze(1).to_broadcast([P, 4, 64]),
                                in1=t_f[:].unsqueeze(2).to_broadcast([P, 4, 64]), op=ALU.mult)
        nc.vector.tensor_scalar(out=k_i[:], in0=ang[:], scalar1=1.0 / TWO_PI, scalar2=None, op0=ALU.mult)
        nc.vector.tensor_copy(out=k_f[:], in_=k_i[:])
        nc.vector.scalar_tensor_tensor(out=r1[:], in0=k_f[:], scalar=-C1, in1=ang[:], op0=ALU.mult, op1=ALU.add)
        nc.vector.scalar_tensor_tensor(out=r2[:], in0=k_f[:], scalar=-C2, in1=r1[:], op0=ALU.mult, op1=ALU.add)
        nc.vector.tensor_scalar(out=gc[:], in0=r2[:], scalar1=0.5 * math.pi, scalar2=-TWO_PI,
                                op0=ALU.is_gt, op1=ALU.mult)
        nc.vector.tensor_scalar(out=gs[:], in0=r2[:], scalar1=math.pi, scalar2=TWO_PI, op0=ALU.is_gt, op1=ALU.mult)
        nc.vector.tensor_tensor(out=rc[:], in0=r2[:], in1=gc[:], op=ALU.add)
        r2_v = r2[:].rearrange("p j (c e) -> p j c e", e=2)
        gs_v = gs[:].rearrange("p j (c e) -> p j c e", e=2)
        rs_v = rs[:].rearrange("p j (c e) -> p j c e", e=2)
        nc.gpsimd.tensor_tensor(out=rs_v[:, :, :, 0], in0=r2_v[:, :, :, 1], in1=gs_v[:, :, :, 1], op=ALU.subtract)
        nc.gpsimd.tensor_tensor(out=rs_v[:, :, :, 1], in0=gs_v[:, :, :, 0], in1=r2_v[:, :, :, 0], op=ALU.subtract)

        def words_in(src32, tag, key=None):
            bk = bank(tag)
            for q in range(4):
                first = 2 * P * (q // 2) + q % 2
                words = src32[:, first:first + 2 * P - 1:2]
                if key in ordered:
                    words = ordered[key][:, P * q:P * (q + 1)]
                nc.tensor.transpose(bk[:, P * q:P * (q + 1)], words, ident[:])
            return bk[:].rearrange("p (g u r) -> p g r u", g=2, u=2)

        ordered = {}

        def order_words(key, src, eng):
            ordered[key] = srt.tile([P, 512], F32, name="srt")
            copy_out(eng, ordered[key][:].rearrange("p (g u r) -> p g u r", g=2, u=2),
                     src.bitcast(F32).rearrange("p (g r u) -> p g u r", g=2, u=2))

        def copy_out(eng, out, in_):
            if eng is nc.scalar:
                nc.scalar.copy(out=out, in_=in_)
            else:
                nc.vector.tensor_copy(out=out, in_=in_)

        wg = {}

        def w_in(k, m, tag, eng):
            if m == 0:
                wg[k] = wgp.tile([P, 2048], BF16, name="wg", align_bytes=64)
            src = words_in(w_sb[k][m][:].bitcast(F32), tag, ("w", k, m))
            dst = wg[k][:].bitcast(F32)[:, 512 * m:512 * (m + 1)].rearrange("p (g r u) -> p g r u", g=2, u=2)
            copy_out(eng, dst, src)

        def w_quant(k):
            nc.vector.quantize_mx(out=wcodes[k][:].bitcast(FP8X4), scales=wscales[k][:], in_=wg[k][:])

        def w_quant_half(k, m):
            c0 = 256 * m
            nc.vector.quantize_mx(out=wcodes[k][:, c0:c0 + 256].bitcast(FP8X4), scales=wscales[k][:, c0:c0 + 256],
                                  in_=wg[k][:, 4 * c0:4 * (c0 + 256)])

        def x_in(n, j, tag, eng):
            src = words_in(x_sb[n][j][:].bitcast(F32), tag, ("x", n, j))
            copy_out(eng, xg[n][j][:].bitcast(F32).rearrange("p (g c u) -> p g c u", g=2, u=2), src)

        def x_quant(n, j):
            for g in range(2):
                c0 = 512 * g + P * j
                nc.vector.quantize_mx(out=xcodes[n][:, c0:c0 + P].bitcast(FP8X4), scales=xscales[n][:, c0:c0 + P],
                                      in_=xg[n][j][:, 512 * g:512 * (g + 1)])

        rounds = [(k, n) for n in range(2) for k in range(4)] + [(k, n) for k in range(4, 8) for n in range(2)]
        acc = {}
        prod = {}
        ob = {}

        def mx(r, m):
            k, n = rounds[r]
            acc[(r, m)] = bank("A%d" % m)
            for g in range(2):
                s0 = P * (2 * m + g)
                nc.tensor.matmul_mx(out=acc[(r, m)][:],
                                    lhsT=wcodes[k][:, s0:s0 + P].bitcast(FP8X4), lhsT_scale=wscales[k][:, s0:s0 + P],
                                    rhs=xcodes[n][:, 512 * g:512 * (g + 1)].bitcast(FP8X4),
                                    rhs_scale=xscales[n][:, 512 * g:512 * (g + 1)],
                                    start=(g == 0), stop=(g == 1))

        def bias_of(r, m):
            head = 2 * rounds[r][0] + m
            return bias_sb[:, head:head + 1]

        def products(r, m):
            prod[(r, m)] = abp.tile([P, 2, 512], F32, name="ab")
            nc.vector.scalar_tensor_tensor(out=prod[(r, m)][:],
                                           in0=acc[(r, m)][:].unsqueeze(1).to_broadcast([P, 2, 512]),
                                           scalar=bias_of(r, m), in1=chan[:], op0=ALU.add, op1=ALU.mult)

        def back(r, m):
            bk = bank("O%d%d" % (r % 2, m))
            for j in range(4):
                cols = slice(P * j, P * (j + 1))
                nc.tensor.matmul(bk[:, cols], lhsT=prod[(r, m)][:, 0, cols], rhs=ident[:], is_transpose=True,
                                 start=True, stop=False)
                nc.tensor.matmul(bk[:, cols], lhsT=prod[(r, m)][:, 1, cols], rhs=swap[:], is_transpose=True,
                                 start=False, stop=True)
            ob[(r, m)] = obp.tile([P, 512], F32, name="ob")
            return bk

        def finish(r, m, bk, eng):
            copy_out(eng, ob[(r, m)][:], bk[:])
            store(r, m)

        def store(r, m):
            k, n = rounds[r]
            nc.sync.dma_start(out=outs[k // 4][n, 2 * (k % 4) + m].rearrange("(p j) d -> p (j d)", j=4),
                              in_=ob[(r, m)][:])

        biased = {}

        def bias_out(r, m):
            biased[(r, m)] = qsp.tile([P, 512], F32, name="qs")
            nc.scalar.activation(out=biased[(r, m)][:], in_=acc[(r, m)][:], func=ACT.Identity, bias=bias_of(r, m),
                                 scale=1.0)

        def back_plain(r, m):
            bk = bank("O%d%d" % (r % 2, m))
            for j in range(4):
                cols = slice(P * j, P * (j + 1))
                nc.tensor.transpose(bk[:, cols], biased[(r, m)][:, cols], ident[:])
            return bk

        def products_plain(r, m, bk):
            prod[(r, m)] = abp.tile([P, 2, 512], F32, name="ab")
            nc.vector.tensor_tensor(out=prod[(r, m)][:], in0=bk[:].unsqueeze(1).to_broadcast([P, 2, 512]),
                                    in1=tok[:].rearrange("p a j h c -> p a (j h c)"), op=ALU.mult)

        def add_plain(r, m, eng):
            ob[(r, m)] = obp.tile([P, 512], F32, name="ob")
            eng.tensor_tensor(out=ob[(r, m)][:].rearrange("p (c e) -> p c e", e=2),
                              in0=prod[(r, m)][:, 0, :].rearrange("p (c e) -> p c e", e=2),
                              in1=prod[(r, m)][:, 1, :].rearrange("p (c e) -> p c e", e=2)[:, :, ::-1], op=ALU.add)
            store(r, m)

        def bias_cast():
            nc.vector.tensor_copy(out=bf[:], in_=bz[:])

        def bias_columns(tag):
            bk = bank(tag)
            nc.tensor.transpose(bk[:, 0:P], bf[:], ident[:])
            nc.scalar.copy(out=bias_sb[:], in_=bk[:, 0:16])

        def sine_table(a):
            if a == 0:
                nc.scalar.activation(out=tok[:, 0], in_=rc[:].unsqueeze(2).to_broadcast([P, 4, 2, 64]), func=ACT.Sin,
                                     bias=half_pi[:, 0:1])
            else:
                nc.scalar.activation(out=tok[:, 1], in_=rs[:].unsqueeze(2).to_broadcast([P, 4, 2, 64]), func=ACT.Sin)

        def chan_table(a, tag, eng):
            bk = bank(tag)
            for j in range(4):
                nc.tensor.transpose(bk[:, P * j:P * (j + 1)], tok[:, a, j].rearrange("p h c -> p (h c)"), ident[:])
            copy_out(eng, chan[:, a, :], bk[:])

        x_in(0, 0, "O00", S)
        sine_table(0)
        x_in(0, 1, "O01", V)
        x_quant(0, 0)
        x_quant(0, 1)
        w_in(0, 0, "IN0", S)
        w_in(0, 1, "IN1", V)
        x_in(0, 2, "O10", S)
        bias_cast()
        w_quant(0)
        x_in(0, 3, "O11", S)
        sine_table(1)
        x_quant(0, 2)
        x_quant(0, 3)
        w_in(1, 0, "IN0", V)
        w_in(1, 1, "IN1", V)
        w_quant(1)
        bias_columns("A1")
        units = [("w", 2, 0), ("w", 2, 1), ("w", 3, 0), ("w", 3, 1)] + [("x", 1, j) for j in range(4)]
        units = units + [("w", k, m) for k in range(4, 8) for m in range(2)]
        done = []
        bks = {}

        def order(i, eng):
            if i < len(units):
                what, a, b = units[i]
                order_words(units[i], w_sb[a][b][:] if what == "w" else x_sb[a][b][:], eng)

        def unit(count=1):
            for i in range(count):
                if len(done) < len(units):
                    what, a, b = units[len(done)]
                    if what == "w":
                        w_in(a, b, "IN%d" % (len(done) % 2), S)
                    else:
                        x_in(a, b, "IN%d" % (len(done) % 2), S)
                    done.append(0)

        def turn(r, m):
            bks[(r, m)] = back_plain(r, m)

        def rotate(r, m):
            products_plain(r, m, bks[(r, m)])
            add_plain(r, m, V if r == 15 and m == 1 or r == 14 and m == 1 else G)

        LAG = 11
        for r in range(16):
            for m in range(2):
                mx(r, m)
                bias_out(r, m)
            if r < LAG:
                unit(1)
                turn(r, 0)
                if r == 3:
                    x_quant(1, 2)
                    x_quant(1, 3)
                rotate(r, 0)
                if r == 2:
                    x_quant(1, 0)
                unit(0 if r > 3 else 2 if r == 2 else 1)
                turn(r, 1)
                rotate(r, 1)
                if r < 2:
                    w_quant(2 + r)
                if r == 2:
                    x_quant(1, 1)
                if r in (5, 7, 9, 11):
                    w_quant((r + 3) // 2)
                if r >= 2:
                    order(6 + r, S)
            else:
                if r > LAG:
                    for m in range(2):
                        turn(r - 1, m)
                unit(1)
                order(r + 6, S)
                if r > LAG:
                    rotate(r - 1, 0)
                if r in (5, 7, 9, 11):
                    w_quant((r + 3) // 2)
                if r > LAG:
                    rotate(r - 1, 1)
        for m in range(2):
            turn(15, m)
            rotate(15, m)
